import numpy as np
import ml_dtypes


BF16 = ml_dtypes.bfloat16


def bf(x):
    return np.asarray(x, np.float32).astype(BF16)


def f64(x):
    return np.asarray(x).astype(np.float64)


E2M1 = np.array([0.0, 0.5, 1.0, 1.5, 2.0, 3.0, 4.0, 6.0, -0.0, -0.5, -1.0, -1.5, -2.0, -3.0, -4.0, -6.0])


def pack_weight(w, fmt):
    k, n = w.shape
    w = f64(bf(w)).reshape(k // 32, 32, n)
    amax = np.abs(w).max(1)
    if fmt == "e4m3":
        byte = np.frexp(amax)[1] - 1 + 127 - 7
    else:
        mant, ex = np.frexp(amax / 6.0)
        byte = np.where(mant > 0.5, ex, ex - 1) + 127
    byte = np.clip(np.where(amax > 0, byte, 1), 1, 254)
    scaled = (w * np.exp2(127.0 - byte)[:, None, :]).reshape(k, n).astype(np.float32)
    by_word = np.ascontiguousarray(scaled.reshape(k // 512, 128, 4, n).transpose(0, 1, 3, 2))
    if fmt == "e4m3":
        words = by_word.astype(ml_dtypes.float8_e4m3fn).view(np.uint8)
    else:
        c = by_word.astype(ml_dtypes.float4_e2m1fn).view(np.uint8) & 0xF
        words = c[..., 0::2] | (c[..., 1::2] << 4)
    return np.ascontiguousarray(words), np.ascontiguousarray(byte.astype(np.uint8).reshape(k // 512, 16, n))


def unpack_weight(words, scales, fmt):
    g, p, n, _ = words.shape
    if fmt == "e4m3":
        vals = np.ascontiguousarray(words).view(ml_dtypes.float8_e4m3fn).astype(np.float64)
    else:
        nib = np.empty((g, p, n, 4), np.uint8)
        nib[..., 0::2] = words & 0xF
        nib[..., 1::2] = words >> 4
        vals = E2M1[nib]
    vals = vals * np.repeat(np.exp2(scales.astype(np.float64) - 127.0), 8, axis=1)[..., None]
    return vals.transpose(0, 1, 3, 2).reshape(g * 512, n)

def pack4(w):
    words, scales = pack_weight(w, "e2m1")
    return words.reshape(words.shape[0], 128, -1), scales


def unpack4(words, scales):
    return unpack_weight(words.reshape(words.shape[0], 128, -1, 2), scales, "e2m1")


def kspread(k):
    return np.exp2(np.repeat(np.random.randint(-6, 7, k // 32), 32).astype(np.float64))


B, S, D, H, HKV, HD, WINDOW, KB = 1, 512, 1536, 16, 8, 128, 256, 512
EPS = 1e-6
THETA = 10000.0


def rope_tables():
    inv_freq = 1.0 / THETA ** (np.arange(0, HD, 2) / HD)
    ang = np.arange(S)[:, None] * inv_freq[None, :]
    emb = np.concatenate([ang, ang], axis=-1)
    return np.broadcast_to(np.cos(emb)[None], (B, S, HD)), np.broadcast_to(np.sin(emb)[None], (B, S, HD))


def rms_norm(x, gain):
    var = np.mean(x * x, axis=-1, keepdims=True)
    return x * (1.0 / np.sqrt(var + EPS)) * gain


def rotate_half(x):
    return np.concatenate([-x[..., HD // 2:], x[..., :HD // 2]], axis=-1)


def apply_rope(x, cos, sin):
    return x * cos[:, :, None, :] + rotate_half(x) * sin[:, :, None, :]


def setup_inputs():
    s = kspread(D)
    cos, sin = rope_tables()
    hidden_states = np.random.standard_normal((B, S, D)) * s
    hidden_states_words, hidden_states_scales = pack4(hidden_states.reshape(B * S, D).T)
    Wq_words, Wq_scales = pack4(np.random.standard_normal((D, H * HD)) / np.sqrt(D) / s[:, None])
    Wk_words, Wk_scales = pack4(np.random.standard_normal((D, HKV * HD)) / np.sqrt(D) / s[:, None])
    Wv_words, Wv_scales = pack4(np.random.standard_normal((D, HKV * HD)) * 2.0 / np.sqrt(D) / s[:, None])
    q_scale = bf(np.random.uniform(0.5, 1.5, HD))
    k_scale = bf(np.random.uniform(0.5, 1.5, HD))
    return {
        "hidden_states_words": hidden_states_words,
        "hidden_states_scales": hidden_states_scales,
        "cos": bf(cos),
        "sin": bf(sin),
        "Wq_words": Wq_words,
        "Wq_scales": Wq_scales,
        "Wk_words": Wk_words,
        "Wk_scales": Wk_scales,
        "Wv_words": Wv_words,
        "Wv_scales": Wv_scales,
        "q_scale": q_scale,
        "k_scale": k_scale,
    }


def reference(hidden_states_words, hidden_states_scales, cos, sin, Wq_words, Wq_scales, Wk_words, Wk_scales, Wv_words, Wv_scales, q_scale, k_scale):
    xq = unpack4(hidden_states_words, hidden_states_scales).T.reshape(B, S, D)
    q = (xq @ unpack4(Wq_words, Wq_scales)).reshape(B, S, H, HD)
    k = (xq @ unpack4(Wk_words, Wk_scales)).reshape(B, S, HKV, HD)
    v = (xq @ unpack4(Wv_words, Wv_scales)).reshape(B, S, HKV, HD)
    q = rms_norm(q, f64(q_scale))
    k = rms_norm(k, f64(k_scale))
    q = apply_rope(q, f64(cos), f64(sin))
    k = apply_rope(k, f64(cos), f64(sin))
    return q, k, v

@@ -1,0 +1,208 @@
+from contextlib import ExitStack
+
+import concourse.mybir as mybir
+
+F32 = mybir.dt.float32
+BF16 = mybir.dt.bfloat16
+I32 = mybir.dt.int32
+U8 = mybir.dt.uint8
+FP4X4 = mybir.dt.float4_e2m1fn_x4
+MULT = mybir.AluOpType.mult
+ADD = mybir.AluOpType.add
+ACT = mybir.ActivationFunctionType
+
+P = 128
+TOKENS, K = 512, 1536
+HEAD = 128
+HALF = HEAD // 2
+PASSES = K // 512
+TILES = TOKENS // P
+N = 512
+HEADS = N // HEAD
+EPS = 1e-6
+FLOPS = 2 * TOKENS * K * 4096
+
+
+def tile_multiheadattention_pa_kernel(
+    tc,
+    hidden_states_words,
+    hidden_states_scales,
+    cos,
+    sin,
+    Wq_words,
+    Wq_scales,
+    Wk_words,
+    Wk_scales,
+    Wv_words,
+    Wv_scales,
+    q_scale,
+    k_scale,
+    out_0,
+    out_1,
+    out_2,
+):
+    nc = tc.nc
+    with ExitStack() as ctx:
+        keep = ctx.enter_context(tc.tile_pool(name="keep", bufs=1))
+        work = ctx.enter_context(tc.tile_pool(name="work", bufs=4))
+        res = ctx.enter_context(tc.tile_pool(name="res", bufs=8))
+        psum = ctx.enter_context(tc.psum_pool(name="psum", bufs=8))
+        ctx.enter_context(tc.manual_schedule())
+
+        def operand(name, width):
+            codes = keep.tile([P, PASSES, 2 * width], U8, name=name + "_codes", align_bytes=64)
+            planes = keep.tile([P, PASSES, width], U8, name=name + "_planes", align_bytes=64)
+            return codes, planes
+
+        def zero(engine, planes):
+            engine.memset(planes[:].rearrange("p g n -> p (g n)").bitcast(I32), 0)
+
+        def load_codes(codes, words, c0, c1):
+            nc.sync.dma_start(
+                out=codes[:].bitcast(I32),
+                in_=words[:, :, 2 * c0 : 2 * c1].rearrange("g p n -> p g n").bitcast(I32),
+            )
+
+        def load_scales(planes, scales, c0, c1):
+            for quad in range(4):
+                nc.sync.dma_start(
+                    out=planes[32 * quad : 32 * quad + 4, :, :].bitcast(I32),
+                    in_=scales[:, 4 * quad : 4 * quad + 4, c0:c1].rearrange("g r n -> r g n").bitcast(I32),
+                )
+
+        x_codes, x_planes = operand("x", TOKENS)
+        q0_codes, q0_planes = operand("q0", N)
+        q1_codes, q1_planes = operand("q1", N)
+        q2_codes, q2_planes = operand("q2", 2 * N)
+        v_codes, v_planes = operand("v", 2 * N)
+        k_codes, k_planes = operand("k", 2 * N)
+
+        gain_rows = keep.tile([P, 2 * HEAD], BF16, name="gain_rows")
+        ones = keep.tile([P, P], BF16, name="ones")
+        cos_sb = keep.tile([P, TILES, HEAD], BF16, name="cos_sb")
+        sin_sb = keep.tile([P, TILES, HEAD], BF16, name="sin_sb")
+        warm = keep.tile([P, 1], F32, name="warm")
+
+        nc.gpsimd.memset(warm[:], 1.0)
+        nc.scalar.activation(out=warm[:], in_=warm[:], func=ACT.Abs_reciprocal_sqrt)
+
+        zero(nc.vector, x_planes)
+        zero(nc.vector, q0_planes)
+        load_codes(x_codes, hidden_states_words, 0, TOKENS)
+        load_codes(q0_codes, Wq_words, 0, N)
+        load_scales(x_planes, hidden_states_scales, 0, TOKENS)
+        load_scales(q0_planes, Wq_scales, 0, N)
+
+        nc.gpsimd.memset(gain_rows[:], 0.0)
+        nc.gpsimd.memset(ones[:], 1.0)
+        nc.gpsimd.dma_start(out=gain_rows[0:1, 0:HEAD], in_=q_scale.unsqueeze(0))
+        nc.gpsimd.dma_start(out=gain_rows[0:1, HEAD : 2 * HEAD], in_=k_scale.unsqueeze(0))
+        nc.gpsimd.dma_start(out=cos_sb[:], in_=cos[0].rearrange("(t p) d -> p t d", p=P))
+        nc.gpsimd.dma_start(out=sin_sb[:], in_=sin[0].rearrange("(t p) d -> p t d", p=P))
+
+        zero(nc.vector, q1_planes)
+        zero(nc.vector, v_planes)
+        zero(nc.vector, q2_planes)
+        zero(nc.vector, k_planes)
+        load_codes(q1_codes, Wq_words, N, 2 * N)
+        load_scales(q1_planes, Wq_scales, N, 2 * N)
+        load_codes(v_codes, Wv_words, 0, 2 * N)
+        load_scales(v_planes, Wv_scales, 0, 2 * N)
+        load_codes(q2_codes, Wq_words, 2 * N, 4 * N)
+        load_scales(q2_planes, Wq_scales, 2 * N, 4 * N)
+        load_codes(k_codes, Wk_words, 0, 2 * N)
+        load_scales(k_planes, Wk_scales, 0, 2 * N)
+
+        gain_ps = psum.tile([P, N], F32, name="acc")
+        nc.tensor.matmul(gain_ps[:, : 2 * HEAD], lhsT=ones[:], rhs=gain_rows[:], start=True, stop=True)
+
+        tables = []
+        for which in range(2):
+            c_tab = keep.tile([P, TILES, HEAD], F32, name="c_tab%d" % which)
+            s_tab = keep.tile([P, TILES, HEAD], F32, name="s_tab%d" % which)
+            gain = gain_ps[:, which * HEAD : (which + 1) * HEAD]
+            nc.vector.tensor_tensor(
+                out=c_tab[:], in0=cos_sb[:], in1=gain.unsqueeze(1).to_broadcast([P, TILES, HEAD]), op=MULT
+            )
+            nc.vector.scalar_tensor_tensor(
+                out=s_tab[:, :, :HALF],
+                in0=sin_sb[:, :, :HALF],
+                scalar=-1.0,
+                in1=gain[:, HALF:].unsqueeze(1).to_broadcast([P, TILES, HALF]),
+                op0=MULT,
+                op1=MULT,
+            )
+            nc.vector.tensor_tensor(
+                out=s_tab[:, :, HALF:],
+                in0=sin_sb[:, :, HALF:],
+                in1=gain[:, :HALF].unsqueeze(1).to_broadcast([P, TILES, HALF]),
+                op=MULT,
+            )
+            tables.append((c_tab, s_tab))
+
+        out_q = out_0.rearrange("b s h d -> (b s) (h d)")
+        out_k = out_1.rearrange("b s h d -> (b s) (h d)")
+        out_v = out_2.rearrange("b s h d -> (b s) (h d)")
+
+        rope_units = [
+            (q0_codes, q0_planes, 0, out_q, 0, 0),
+            (q1_codes, q1_planes, 0, out_q, 1, 0),
+            (q2_codes, q2_planes, 0, out_q, 2, 0),
+            (q2_codes, q2_planes, 1, out_q, 3, 0),
+            (k_codes, k_planes, 0, out_k, 0, 1),
+            (k_codes, k_planes, 1, out_k, 1, 1),
+        ]
+        rope_groups = [(unit, t) for unit in rope_units for t in range(TILES)]
+        v_groups = [((v_codes, v_planes, b, out_v, b, None), t) for b in range(2) for t in range(TILES)]
+        order = []
+        for i, group in enumerate(rope_groups):
+            order.append(group)
+            if i % 3 == 0 and i > 0:
+                order.append(v_groups[i // 3 - 1])
+        order.append(v_groups[-1])
+
+        for (codes, planes, b, out, block, which), t in order:
+            acc = psum.tile([P, N], F32, name="acc")
+            for g in range(PASSES):
+                nc.tensor.matmul_mx(
+                    acc[:],
+                    lhsT=x_codes[:, g, 2 * P * t : 2 * P * (t + 1)].bitcast(FP4X4),
+                    lhsT_scale=x_planes[:, g, P * t : P * (t + 1)],
+                    rhs=codes[:, g, 2 * N * b : 2 * N * (b + 1)].bitcast(FP4X4),
+                    rhs_scale=planes[:, g, N * b : N * (b + 1)],
+                    start=(g == 0),
+                    stop=(g == PASSES - 1),
+                )
+            r = res.tile([P, N], F32, name="r")
+            if which is None:
+                nc.scalar.copy(out=r[:], in_=acc[:])
+            else:
+                c_tab, s_tab = tables[which]
+                junk = work.tile([P, N], F32, name="junk")
+                ss = work.tile([P, HEADS], F32, name="ss")
+                inv = work.tile([P, HEADS], F32, name="inv")
+                for h in range(HEADS):
+                    cols = slice(h * HEAD, (h + 1) * HEAD)
+                    nc.scalar.activation(
+                        out=junk[:, cols], in_=acc[:, cols], func=ACT.Square, accum_out=ss[:, h : h + 1]
+                    )
+                nc.scalar.activation(
+                    out=inv[:], in_=ss[:], func=ACT.Abs_reciprocal_sqrt, scale=1.0 / HEAD, bias=EPS
+                )
+                a = work.tile([P, N], F32, name="a")
+                bb = work.tile([P, N], F32, name="bb")
+                for h in range(HEADS):
+                    cols = slice(h * HEAD, (h + 1) * HEAD)
+                    nc.vector.scalar_tensor_tensor(
+                        out=a[:, cols], in0=acc[:, cols], scalar=inv[:, h : h + 1], in1=c_tab[:, t, :], op0=MULT, op1=MULT
+                    )
+                    nc.vector.scalar_tensor_tensor(
+                        out=bb[:, cols].rearrange("p (s d) -> p s d", s=2),
+                        in0=acc[:, cols].rearrange("p (s d) -> p s d", s=2)[:, ::-1, :],
+                        scalar=inv[:, h : h + 1],
+                        in1=s_tab[:, t, :].rearrange("p (s d) -> p s d", s=2),
+                        op0=MULT,
+                        op1=MULT,
+                    )
+                nc.gpsimd.tensor_tensor(out=r[:], in0=a[:], in1=bb[:], op=ADD)
+            nc.sync.dma_start(out=out[t * P : (t + 1) * P, block * N : (block + 1) * N], in_=r[:])

@@ -83,22 +83,22 @@ def tile_multiheadattention_pa_kernel(
         sin_sb = keep.tile([P, TILES, HEAD], BF16, name="sin_sb")
         warm = keep.tile([P, 1], F32, name="warm")
 
-        nc.gpsimd.memset(warm[:], 1.0)
-        nc.scalar.activation(out=warm[:], in_=warm[:], func=ACT.Abs_reciprocal_sqrt)
+        nc.gpsimd.memset(gain_rows[:], 0.0)
+        nc.gpsimd.dma_start(out=cos_sb[:], in_=cos[0].rearrange("(t p) d -> p t d", p=P))
+        nc.gpsimd.dma_start(out=sin_sb[:], in_=sin[0].rearrange("(t p) d -> p t d", p=P))
+        nc.gpsimd.memset(ones[:], 1.0)
 
         zero(nc.vector, x_planes)
         zero(nc.vector, q0_planes)
+        nc.scalar.dma_start(out=gain_rows[0:1, 0:HEAD], in_=q_scale.unsqueeze(0))
+        nc.scalar.dma_start(out=gain_rows[0:1, HEAD : 2 * HEAD], in_=k_scale.unsqueeze(0))
         load_codes(x_codes, hidden_states_words, 0, TOKENS)
         load_codes(q0_codes, Wq_words, 0, N)
         load_scales(x_planes, hidden_states_scales, 0, TOKENS)
         load_scales(q0_planes, Wq_scales, 0, N)
 
-        nc.gpsimd.memset(gain_rows[:], 0.0)
-        nc.gpsimd.memset(ones[:], 1.0)
-        nc.gpsimd.dma_start(out=gain_rows[0:1, 0:HEAD], in_=q_scale.unsqueeze(0))
-        nc.gpsimd.dma_start(out=gain_rows[0:1, HEAD : 2 * HEAD], in_=k_scale.unsqueeze(0))
-        nc.gpsimd.dma_start(out=cos_sb[:], in_=cos[0].rearrange("(t p) d -> p t d", p=P))
-        nc.gpsimd.dma_start(out=sin_sb[:], in_=sin[0].rearrange("(t p) d -> p t d", p=P))
+        nc.gpsimd.memset(warm[:], 1.0)
+        nc.scalar.activation(out=warm[:], in_=warm[:], func=ACT.Abs_reciprocal_sqrt)
 
         zero(nc.vector, q1_planes)
         zero(nc.vector, v_planes)
@@ -154,14 +154,9 @@ def tile_multiheadattention_pa_kernel(
         ]
         rope_groups = [(unit, t) for unit in rope_units for t in range(TILES)]
         v_groups = [((v_codes, v_planes, b, out_v, b, None), t) for b in range(2) for t in range(TILES)]
-        order = []
-        for i, group in enumerate(rope_groups):
-            order.append(group)
-            if i % 3 == 0 and i > 0:
-                order.append(v_groups[i // 3 - 1])
-        order.append(v_groups[-1])
 
-        for (codes, planes, b, out, block, which), t in order:
+        def multiply(group):
+            (codes, planes, b, out, block, which), t = group
             acc = psum.tile([P, N], F32, name="acc")
             for g in range(PASSES):
                 nc.tensor.matmul_mx(
@@ -173,36 +168,104 @@ def tile_multiheadattention_pa_kernel(
                     start=(g == 0),
                     stop=(g == PASSES - 1),
                 )
-            r = res.tile([P, N], F32, name="r")
-            if which is None:
-                nc.scalar.copy(out=r[:], in_=acc[:])
-            else:
-                c_tab, s_tab = tables[which]
-                junk = work.tile([P, N], F32, name="junk")
-                ss = work.tile([P, HEADS], F32, name="ss")
-                inv = work.tile([P, HEADS], F32, name="inv")
-                for h in range(HEADS):
-                    cols = slice(h * HEAD, (h + 1) * HEAD)
-                    nc.scalar.activation(
-                        out=junk[:, cols], in_=acc[:, cols], func=ACT.Square, accum_out=ss[:, h : h + 1]
-                    )
+            return acc
+
+        def store(group, r, c0, c1):
+            (codes, planes, b, out, block, which), t = group
+            nc.sync.dma_start(out=out[t * P : (t + 1) * P, block * N + c0 : block * N + c1], in_=r)
+
+        def squares(acc, ss, first):
+            junk = work.tile([P, N], F32, name="junk")
+            for h in range(HEADS):
+                cols = slice(h * HEAD, (h + 1) * HEAD)
                 nc.scalar.activation(
-                    out=inv[:], in_=ss[:], func=ACT.Abs_reciprocal_sqrt, scale=1.0 / HEAD, bias=EPS
+                    out=junk[:, cols], in_=acc[:, cols], func=ACT.Square, accum_out=ss[:, first + h : first + h + 1]
                 )
-                a = work.tile([P, N], F32, name="a")
-                bb = work.tile([P, N], F32, name="bb")
-                for h in range(HEADS):
-                    cols = slice(h * HEAD, (h + 1) * HEAD)
-                    nc.vector.scalar_tensor_tensor(
-                        out=a[:, cols], in0=acc[:, cols], scalar=inv[:, h : h + 1], in1=c_tab[:, t, :], op0=MULT, op1=MULT
-                    )
-                    nc.vector.scalar_tensor_tensor(
-                        out=bb[:, cols].rearrange("p (s d) -> p s d", s=2),
-                        in0=acc[:, cols].rearrange("p (s d) -> p s d", s=2)[:, ::-1, :],
-                        scalar=inv[:, h : h + 1],
-                        in1=s_tab[:, t, :].rearrange("p (s d) -> p s d", s=2),
-                        op0=MULT,
-                        op1=MULT,
-                    )
-                nc.gpsimd.tensor_tensor(out=r[:], in0=a[:], in1=bb[:], op=ADD)
-            nc.sync.dma_start(out=out[t * P : (t + 1) * P, block * N : (block + 1) * N], in_=r[:])
+
+        def products(group, acc):
+            c_tab, s_tab = tables[group[0][5]]
+            t = group[1]
+            a = work.tile([P, N], F32, name="a")
+            b = work.tile([P, N], F32, name="b")
+            nc.vector.tensor_tensor(
+                out=a[:].rearrange("p (h d) -> p h d", d=HEAD),
+                in0=acc[:].rearrange("p (h d) -> p h d", d=HEAD),
+                in1=c_tab[:, t, :].unsqueeze(1).to_broadcast([P, HEADS, HEAD]),
+                op=MULT,
+            )
+            nc.vector.tensor_tensor(
+                out=b[:].rearrange("p (h s d) -> p h s d", s=2, d=HALF),
+                in0=acc[:].rearrange("p (h s d) -> p h s d", s=2, d=HALF)[:, :, ::-1, :],
+                in1=s_tab[:, t, :].rearrange("p (s d) -> p s d", s=2).unsqueeze(1).to_broadcast([P, HEADS, 2, HALF]),
+                op=MULT,
+            )
+            return a, b
+
+        def normed_products(group, acc, inv, first):
+            c_tab, s_tab = tables[group[0][5]]
+            t = group[1]
+            a = work.tile([P, N], F32, name="a")
+            b = work.tile([P, N], F32, name="b")
+            for h in range(HEADS):
+                cols = slice(h * HEAD, (h + 1) * HEAD)
+                factor = inv[:, first + h : first + h + 1]
+                nc.vector.scalar_tensor_tensor(
+                    out=a[:, cols], in0=acc[:, cols], scalar=factor, in1=c_tab[:, t, :], op0=MULT, op1=MULT
+                )
+                nc.vector.scalar_tensor_tensor(
+                    out=b[:, cols].rearrange("p (s d) -> p s d", s=2),
+                    in0=acc[:, cols].rearrange("p (s d) -> p s d", s=2)[:, ::-1, :],
+                    scalar=factor,
+                    in1=s_tab[:, t, :].rearrange("p (s d) -> p s d", s=2),
+                    op0=MULT,
+                    op1=MULT,
+                )
+            return a, b
+
+        def scale_and_store(group, total, inv):
+            r = res.tile([P, N], F32, name="r")
+            for h in range(HEADS):
+                cols = slice(h * HEAD, (h + 1) * HEAD)
+                nc.scalar.activation(out=r[:, cols], in_=total[:, cols], func=ACT.Copy, scale=inv[:, h : h + 1])
+            store(group, r[:], 0, N)
+
+        pairs = len(rope_groups) // 2
+        pending = None
+        for p in range(pairs):
+            late, early = rope_groups[2 * p], rope_groups[2 * p + 1]
+            acc_late = multiply(late)
+            acc_early = multiply(early)
+            ss = work.tile([P, 2 * HEADS], F32, name="ss")
+            inv = work.tile([P, 2 * HEADS], F32, name="inv")
+            squares(acc_late, ss, 0)
+            squares(acc_early, ss, HEADS)
+            if pending is not None:
+                scale_and_store(*pending)
+            nc.scalar.activation(out=inv[:], in_=ss[:], func=ACT.Abs_reciprocal_sqrt, scale=1.0 / HEAD, bias=EPS)
+
+            a, b = products(late, acc_late)
+            total = work.tile([P, N], F32, name="total")
+            nc.gpsimd.tensor_tensor(out=total[:], in0=a[:], in1=b[:], op=ADD)
+            pending = (late, total, inv)
+
+            a, b = normed_products(early, acc_early, inv, HEADS)
+            if p < pairs - 1:
+                r = res.tile([P, N], F32, name="r")
+                nc.gpsimd.tensor_tensor(out=r[:], in0=a[:], in1=b[:], op=ADD)
+                store(early, r[:], 0, N)
+            else:
+                scale_and_store(*pending)
+                half = N // 2
+                r_low = res.tile([P, half], F32, name="r_low")
+                r_high = res.tile([P, half], F32, name="r_high")
+                nc.gpsimd.tensor_tensor(out=r_low[:], in0=a[:, :half], in1=b[:, :half], op=ADD)
+                store(early, r_low[:], 0, half)
+                nc.vector.tensor_tensor(out=r_high[:], in0=a[:, half:], in1=b[:, half:], op=ADD)
+                store(early, r_high[:], half, N)
+
+            if 1 <= p <= len(v_groups):
+                group = v_groups[p - 1]
+                acc = multiply(group)
+                r = res.tile([P, N], F32, name="r")
+                nc.scalar.copy(out=r[:], in_=acc[:])
+                store(group, r[:], 0, N)

from contextlib import ExitStack

import concourse.mybir as mybir

F32 = mybir.dt.float32
BF16 = mybir.dt.bfloat16
I32 = mybir.dt.int32
U8 = mybir.dt.uint8
FP4X4 = mybir.dt.float4_e2m1fn_x4
MULT = mybir.AluOpType.mult
ADD = mybir.AluOpType.add
ACT = mybir.ActivationFunctionType

P = 128
TOKENS, K = 512, 1536
HEAD = 128
HALF = HEAD // 2
PASSES = K // 512
TILES = TOKENS // P
N = 512
HEADS = N // HEAD
EPS = 1e-6
FLOPS = 2 * TOKENS * K * 4096


def tile_multiheadattention_pa_kernel(
    tc,
    hidden_states_words,
    hidden_states_scales,
    cos,
    sin,
    Wq_words,
    Wq_scales,
    Wk_words,
    Wk_scales,
    Wv_words,
    Wv_scales,
    q_scale,
    k_scale,
    out_0,
    out_1,
    out_2,
):
    nc = tc.nc
    with ExitStack() as ctx:
        keep = ctx.enter_context(tc.tile_pool(name="keep", bufs=1))
        work = ctx.enter_context(tc.tile_pool(name="work", bufs=4))
        res = ctx.enter_context(tc.tile_pool(name="res", bufs=8))
        psum = ctx.enter_context(tc.psum_pool(name="psum", bufs=8))
        ctx.enter_context(tc.manual_schedule())

        def operand(name, width):
            codes = keep.tile([P, PASSES, 2 * width], U8, name=name + "_codes", align_bytes=64)
            planes = keep.tile([P, PASSES, width], U8, name=name + "_planes", align_bytes=64)
            return codes, planes

        def zero(engine, planes):
            engine.memset(planes[:].rearrange("p g n -> p (g n)").bitcast(I32), 0)

        def load_codes(codes, words, c0, c1):
            nc.sync.dma_start(
                out=codes[:].bitcast(I32),
                in_=words[:, :, 2 * c0 : 2 * c1].rearrange("g p n -> p g n").bitcast(I32),
            )

        def load_scales(planes, scales, c0, c1):
            for quad in range(4):
                nc.sync.dma_start(
                    out=planes[32 * quad : 32 * quad + 4, :, :].bitcast(I32),
                    in_=scales[:, 4 * quad : 4 * quad + 4, c0:c1].rearrange("g r n -> r g n").bitcast(I32),
                )

        x_codes, x_planes = operand("x", TOKENS)
        q0_codes, q0_planes = operand("q0", N)
        q1_codes, q1_planes = operand("q1", N)
        q2_codes, q2_planes = operand("q2", 2 * N)
        v_codes, v_planes = operand("v", 2 * N)
        k_codes, k_planes = operand("k", 2 * N)

        gain_rows = keep.tile([P, 2 * HEAD], BF16, name="gain_rows")
        ones = keep.tile([P, P], BF16, name="ones")
        cos_sb = keep.tile([P, TILES, HEAD], BF16, name="cos_sb")
        sin_sb = keep.tile([P, TILES, HEAD], BF16, name="sin_sb")
        warm = keep.tile([P, 1], F32, name="warm")

        nc.gpsimd.memset(gain_rows[:], 0.0)
        nc.gpsimd.dma_start(out=cos_sb[:], in_=cos[0].rearrange("(t p) d -> p t d", p=P))
        nc.gpsimd.dma_start(out=sin_sb[:], in_=sin[0].rearrange("(t p) d -> p t d", p=P))
        nc.gpsimd.memset(ones[:], 1.0)

        zero(nc.vector, x_planes)
        zero(nc.vector, q0_planes)
        nc.scalar.dma_start(out=gain_rows[0:1, 0:HEAD], in_=q_scale.unsqueeze(0))
        nc.scalar.dma_start(out=gain_rows[0:1, HEAD : 2 * HEAD], in_=k_scale.unsqueeze(0))
        load_codes(x_codes, hidden_states_words, 0, TOKENS)
        load_codes(q0_codes, Wq_words, 0, N)
        load_scales(x_planes, hidden_states_scales, 0, TOKENS)
        load_scales(q0_planes, Wq_scales, 0, N)

        nc.gpsimd.memset(warm[:], 1.0)
        nc.scalar.activation(out=warm[:], in_=warm[:], func=ACT.Abs_reciprocal_sqrt)

        zero(nc.vector, q1_planes)
        zero(nc.vector, v_planes)
        zero(nc.vector, q2_planes)
        zero(nc.vector, k_planes)
        load_codes(q1_codes, Wq_words, N, 2 * N)
        load_scales(q1_planes, Wq_scales, N, 2 * N)
        load_codes(v_codes, Wv_words, 0, 2 * N)
        load_scales(v_planes, Wv_scales, 0, 2 * N)
        load_codes(q2_codes, Wq_words, 2 * N, 4 * N)
        load_scales(q2_planes, Wq_scales, 2 * N, 4 * N)
        load_codes(k_codes, Wk_words, 0, 2 * N)
        load_scales(k_planes, Wk_scales, 0, 2 * N)

        gain_ps = psum.tile([P, N], F32, name="acc")
        nc.tensor.matmul(gain_ps[:, : 2 * HEAD], lhsT=ones[:], rhs=gain_rows[:], start=True, stop=True)

        tables = []
        for which in range(2):
            c_tab = keep.tile([P, TILES, HEAD], F32, name="c_tab%d" % which)
            s_tab = keep.tile([P, TILES, HEAD], F32, name="s_tab%d" % which)
            gain = gain_ps[:, which * HEAD : (which + 1) * HEAD]
            nc.vector.tensor_tensor(
                out=c_tab[:], in0=cos_sb[:], in1=gain.unsqueeze(1).to_broadcast([P, TILES, HEAD]), op=MULT
            )
            nc.vector.scalar_tensor_tensor(
                out=s_tab[:, :, :HALF],
                in0=sin_sb[:, :, :HALF],
                scalar=-1.0,
                in1=gain[:, HALF:].unsqueeze(1).to_broadcast([P, TILES, HALF]),
                op0=MULT,
                op1=MULT,
            )
            nc.vector.tensor_tensor(
                out=s_tab[:, :, HALF:],
                in0=sin_sb[:, :, HALF:],
                in1=gain[:, :HALF].unsqueeze(1).to_broadcast([P, TILES, HALF]),
                op=MULT,
            )
            tables.append((c_tab, s_tab))

        out_q = out_0.rearrange("b s h d -> (b s) (h d)")
        out_k = out_1.rearrange("b s h d -> (b s) (h d)")
        out_v = out_2.rearrange("b s h d -> (b s) (h d)")

        rope_units = [
            (q0_codes, q0_planes, 0, out_q, 0, 0),
            (q1_codes, q1_planes, 0, out_q, 1, 0),
            (q2_codes, q2_planes, 0, out_q, 2, 0),
            (q2_codes, q2_planes, 1, out_q, 3, 0),
            (k_codes, k_planes, 0, out_k, 0, 1),
            (k_codes, k_planes, 1, out_k, 1, 1),
        ]
        rope_groups = [(unit, t) for unit in rope_units for t in range(TILES)]
        v_groups = [((v_codes, v_planes, b, out_v, b, None), t) for b in range(2) for t in range(TILES)]

        def multiply(group):
            (codes, planes, b, out, block, which), t = group
            acc = psum.tile([P, N], F32, name="acc")
            for g in range(PASSES):
                nc.tensor.matmul_mx(
                    acc[:],
                    lhsT=x_codes[:, g, 2 * P * t : 2 * P * (t + 1)].bitcast(FP4X4),
                    lhsT_scale=x_planes[:, g, P * t : P * (t + 1)],
                    rhs=codes[:, g, 2 * N * b : 2 * N * (b + 1)].bitcast(FP4X4),
                    rhs_scale=planes[:, g, N * b : N * (b + 1)],
                    start=(g == 0),
                    stop=(g == PASSES - 1),
                )
            return acc

        def store(group, r, c0, c1):
            (codes, planes, b, out, block, which), t = group
            nc.sync.dma_start(out=out[t * P : (t + 1) * P, block * N + c0 : block * N + c1], in_=r)

        def squares(acc, ss, first):
            junk = work.tile([P, N], F32, name="junk")
            for h in range(HEADS):
                cols = slice(h * HEAD, (h + 1) * HEAD)
                nc.scalar.activation(
                    out=junk[:, cols], in_=acc[:, cols], func=ACT.Square, accum_out=ss[:, first + h : first + h + 1]
                )

        def products(group, acc):
            c_tab, s_tab = tables[group[0][5]]
            t = group[1]
            a = work.tile([P, N], F32, name="a")
            b = work.tile([P, N], F32, name="b")
            nc.vector.tensor_tensor(
                out=a[:].rearrange("p (h d) -> p h d", d=HEAD),
                in0=acc[:].rearrange("p (h d) -> p h d", d=HEAD),
                in1=c_tab[:, t, :].unsqueeze(1).to_broadcast([P, HEADS, HEAD]),
                op=MULT,
            )
            nc.vector.tensor_tensor(
                out=b[:].rearrange("p (h s d) -> p h s d", s=2, d=HALF),
                in0=acc[:].rearrange("p (h s d) -> p h s d", s=2, d=HALF)[:, :, ::-1, :],
                in1=s_tab[:, t, :].rearrange("p (s d) -> p s d", s=2).unsqueeze(1).to_broadcast([P, HEADS, 2, HALF]),
                op=MULT,
            )
            return a, b

        def normed_products(group, acc, inv, first):
            c_tab, s_tab = tables[group[0][5]]
            t = group[1]
            a = work.tile([P, N], F32, name="a")
            b = work.tile([P, N], F32, name="b")
            for h in range(HEADS):
                cols = slice(h * HEAD, (h + 1) * HEAD)
                factor = inv[:, first + h : first + h + 1]
                nc.vector.scalar_tensor_tensor(
                    out=a[:, cols], in0=acc[:, cols], scalar=factor, in1=c_tab[:, t, :], op0=MULT, op1=MULT
                )
                nc.vector.scalar_tensor_tensor(
                    out=b[:, cols].rearrange("p (s d) -> p s d", s=2),
                    in0=acc[:, cols].rearrange("p (s d) -> p s d", s=2)[:, ::-1, :],
                    scalar=factor,
                    in1=s_tab[:, t, :].rearrange("p (s d) -> p s d", s=2),
                    op0=MULT,
                    op1=MULT,
                )
            return a, b

        def scale_and_store(group, total, inv):
            r = res.tile([P, N], F32, name="r")
            for h in range(HEADS):
                cols = slice(h * HEAD, (h + 1) * HEAD)
                nc.scalar.activation(out=r[:, cols], in_=total[:, cols], func=ACT.Copy, scale=inv[:, h : h + 1])
            store(group, r[:], 0, N)

        pairs = len(rope_groups) // 2
        pending = None
        for p in range(pairs):
            late, early = rope_groups[2 * p], rope_groups[2 * p + 1]
            acc_late = multiply(late)
            acc_early = multiply(early)
            ss = work.tile([P, 2 * HEADS], F32, name="ss")
            inv = work.tile([P, 2 * HEADS], F32, name="inv")
            squares(acc_late, ss, 0)
            squares(acc_early, ss, HEADS)
            if pending is not None:
                scale_and_store(*pending)
            nc.scalar.activation(out=inv[:], in_=ss[:], func=ACT.Abs_reciprocal_sqrt, scale=1.0 / HEAD, bias=EPS)

            a, b = products(late, acc_late)
            total = work.tile([P, N], F32, name="total")
            nc.gpsimd.tensor_tensor(out=total[:], in0=a[:], in1=b[:], op=ADD)
            pending = (late, total, inv)

            a, b = normed_products(early, acc_early, inv, HEADS)
            if p < pairs - 1:
                r = res.tile([P, N], F32, name="r")
                nc.gpsimd.tensor_tensor(out=r[:], in0=a[:], in1=b[:], op=ADD)
                store(early, r[:], 0, N)
            else:
                scale_and_store(*pending)
                half = N // 2
                r_low = res.tile([P, half], F32, name="r_low")
                r_high = res.tile([P, half], F32, name="r_high")
                nc.gpsimd.tensor_tensor(out=r_low[:], in0=a[:, :half], in1=b[:, :half], op=ADD)
                store(early, r_low[:], 0, half)
                nc.vector.tensor_tensor(out=r_high[:], in0=a[:, half:], in1=b[:, half:], op=ADD)
                store(early, r_high[:], half, N)

            if 1 <= p <= len(v_groups):
                group = v_groups[p - 1]
                acc = multiply(group)
                r = res.tile([P, N], F32, name="r")
                nc.scalar.copy(out=r[:], in_=acc[:])
                store(group, r[:], 0, N)
